import numpy as np
import ml_dtypes


def mxq(x, axis, fmt="e4m3"):
    dtype, down = {"e4m3": (ml_dtypes.float8_e4m3fn, 7), "e5m2": (ml_dtypes.float8_e5m2, 14)}[fmt]
    v = np.moveaxis(np.asarray(x, np.float32).astype(ml_dtypes.bfloat16).astype(np.float64), axis, -1)
    blocks = v.reshape(v.shape[:-1] + (-1, 32))
    amax = np.abs(blocks).max(-1, keepdims=True)
    byte = np.maximum(np.where(amax > 0, np.frexp(amax)[1] - 1 + 127, 0) - down, 1)
    scale = np.exp2(byte - 127.0)
    codes = (blocks / scale).astype(np.float32).astype(dtype).astype(np.float64)
    return np.moveaxis((codes * scale).reshape(v.shape), -1, axis)


WIDE = False


def mx_kscale(k):
    if not WIDE:
        return np.ones(k)
    levels = np.array([10, -10, 5, -5, 0])
    if k % 512:
        return np.exp2(np.random.permutation(np.resize(levels, k // 32))).repeat(32)
    a = np.empty((k // 512, 16))
    for p in range(k // 512):
        a[p, :8] = np.random.permutation(np.resize(levels, 8))
        for g in range(8):
            far = levels[np.abs(levels - a[p, g]) >= 10]
            a[p, g + 8] = far[np.random.randint(len(far))]
    return np.exp2(a.ravel()).repeat(32)


BF16 = ml_dtypes.bfloat16


def bf(x):
    return np.asarray(x, np.float32).astype(BF16)


def f64(x):
    return np.asarray(x).astype(np.float64)


B, L, D, E, W1, C, F_LEN = 2, 1024, 511, 512, 8, 256, 4
SR = 0.55
WS = 0.7
KEEP = 0.75


def setup_inputs():
    s = mx_kscale(E)
    st = np.random.standard_normal((B, L, E)) * SR
    st[..., 0] = 1.0
    return {"state": bf(st * s),
            "Wg": bf(np.random.standard_normal((C, W1, E)) * WS / np.sqrt(E) / s),
            "Mg": bf(np.random.random((C, W1, E)) < KEEP),
            "bg": bf(1.0 + 0.1 * np.random.standard_normal((C, W1)))}


def reference(state, Wg, Mg, bg):
    wm = f64(Wg) * f64(Mg)
    sq = mxq(f64(state).reshape(B * L, E), 1, "e4m3")
    wq = mxq(wm.reshape(C * W1, E), 1, "e4m3")
    h = (sq @ wq.T).reshape(B, L, C, W1) + f64(bg)
    return np.prod(h, axis=-1)

@@ -1,0 +1,220 @@
+from contextlib import ExitStack
+
+import concourse.mybir as mybir
+from concourse.masks import make_identity
+
+F32 = mybir.dt.float32
+BF16 = mybir.dt.bfloat16
+U32 = mybir.dt.uint32
+U8 = mybir.dt.uint8
+FP8X4 = mybir.dt.float8_e4m3fn_x4
+ADD = mybir.AluOpType.add
+MULT = mybir.AluOpType.mult
+IDENTITY = mybir.ActivationFunctionType.Identity
+
+P = 128
+E = 512
+TOKENS = 2048
+CHANNELS = 256
+FORMS = 8
+CHUNK = 512
+CHUNK_ROWS = CHUNK // P
+TOKEN_CHUNKS = TOKENS // CHUNK
+CHANNEL_HALVES = CHANNELS // P
+GROUPS = CHANNEL_HALVES * TOKEN_CHUNKS
+UNIT_ROWS = 2
+UNIT = UNIT_ROWS * P
+FORM_PAIRS = FORMS // UNIT_ROWS
+SCALAR_FORMS = (0, 2, 4)
+VECTOR_FORMS = ((1, 0), (3, 1), (5, 2), (6, 0), (7, 1))
+
+QUANTISE_LAG = 3
+OUT_LAG = 2
+
+FLOPS = 2 * TOKENS * CHANNELS * FORMS * E
+
+
+def tile_ac_filter_prenorm_net_nd_pa_kernel(tc, state, Wg, Mg, bg, out):
+    nc = tc.nc
+    state_rows = state.flatten_outer_dims().rearrange("(q n) e -> q n e", q=P)
+    out_rows = out.flatten_outer_dims().rearrange("(q n) c -> q n c", q=P)
+    wg_rows = Wg.rearrange("(h c) j e -> h c j e", c=P)
+    mg_rows = Mg.rearrange("(h c) j e -> h c j e", c=P)
+
+    with ExitStack() as ctx:
+        ctx.enter_context(tc.manual_schedule())
+        keep = ctx.enter_context(tc.tile_pool(name="keep", bufs=1))
+        chains = ctx.enter_context(tc.tile_pool(name="chains", bufs=OUT_LAG + 2))
+        stage = ctx.enter_context(tc.tile_pool(name="stage", bufs=3))
+        banks = ctx.enter_context(tc.psum_pool(name="banks", bufs=8))
+
+        bias_bf16 = keep.tile([P, CHANNEL_HALVES, FORMS], BF16)
+        nc.scalar.dma_start(out=bias_bf16[:], in_=bg.rearrange("(h c) j -> c h j", c=P))
+
+        state_tiles = {}
+        weight_tiles = {}
+
+        def load_state(chunk):
+            s = keep.tile([P, CHUNK_ROWS, E], BF16, name="s%d" % chunk)
+            nc.sync.dma_start(
+                out=s[:], in_=state_rows[:, chunk * CHUNK_ROWS : (chunk + 1) * CHUNK_ROWS, :]
+            )
+            state_tiles[chunk] = s
+
+        def load_weights(half, pair):
+            forms = slice(pair * UNIT_ROWS, (pair + 1) * UNIT_ROWS)
+            w = keep.tile([P, UNIT_ROWS, E], BF16, name="w%d%d" % (half, pair))
+            m = keep.tile([P, UNIT_ROWS, E], BF16, name="m%d%d" % (half, pair))
+            nc.sync.dma_start(out=w[:], in_=wg_rows[half, :, forms, :])
+            nc.sync.dma_start(out=m[:], in_=mg_rows[half, :, forms, :])
+            weight_tiles[(half, pair)] = (w, m)
+
+        load_state(0)
+        load_weights(0, 0)
+        load_weights(0, 1)
+        load_state(1)
+        load_weights(0, 2)
+        load_weights(0, 3)
+        load_state(2)
+        load_state(3)
+        for pair in range(FORM_PAIRS):
+            load_weights(1, pair)
+
+        identity = keep.tile([P, P], F32)
+        make_identity(nc, identity[:])
+        bias = keep.tile([P, CHANNEL_HALVES * FORMS], F32)
+        nc.vector.tensor_copy(out=bias[:], in_=bias_bf16[:].rearrange("c h j -> c (h j)"))
+
+        w_codes = keep.tile([P, CHANNEL_HALVES * FORMS * P], U32, align_bytes=64)
+        w_scales = keep.tile([P, CHANNEL_HALVES * FORMS * P], U8, align_bytes=64)
+        s_codes = keep.tile([P, TOKENS], U32, align_bytes=64)
+        s_scales = keep.tile([P, TOKENS], U8, align_bytes=64)
+
+        grouped_tiles = {}
+
+        def mask(unit):
+            kind, half, pair = unit
+            if kind == "weights":
+                w, m = weight_tiles[(half, pair)]
+                nc.vector.tensor_tensor(out=w[:], in0=w[:], in1=m[:], op=MULT)
+
+        def turn(unit):
+            kind, i, k = unit
+            if kind == "state":
+                rows = state_tiles[i][:, k * UNIT_ROWS : (k + 1) * UNIT_ROWS, :]
+            else:
+                rows = weight_tiles[(i, k)][0][:]
+            words = rows.bitcast(F32)
+            turned = banks.tile([P, UNIT_ROWS, 2, P], F32, tag="bank")
+            for a in range(UNIT_ROWS):
+                for u in range(2):
+                    nc.tensor.transpose(turned[:, a, u, :], words[:, a, u : UNIT : 2], identity[:])
+            grouped = keep.tile([P, UNIT_ROWS, P, 4], BF16, name="grouped_%s%d%d" % unit, align_bytes=64)
+            nc.scalar.copy(out=grouped[:].bitcast(F32), in_=turned[:].rearrange("p a u r -> p a r u"))
+            grouped_tiles[unit] = grouped
+
+        def quantise(unit):
+            kind, i, k = unit
+            codes, scales = (s_codes, s_scales) if kind == "state" else (w_codes, w_scales)
+            units_before = i * (CHUNK // UNIT) + k if kind == "state" else i * FORM_PAIRS + k
+            columns = slice(units_before * UNIT, (units_before + 1) * UNIT)
+            nc.vector.quantize_mx(
+                out=codes[:, columns].bitcast(FP8X4),
+                scales=scales[:, columns],
+                in_=grouped_tiles[unit][:].rearrange("p a r t -> p (a r t)"),
+            )
+
+        def form_pass(group, j):
+            half, chunk = divmod(group, TOKEN_CHUNKS)
+            w_columns = slice((half * FORMS + j) * P, (half * FORMS + j + 1) * P)
+            s_columns = slice(chunk * CHUNK, (chunk + 1) * CHUNK)
+            bank = banks.tile([P, CHUNK], F32, tag="bank")
+            nc.tensor.matmul_mx(
+                out=bank[:],
+                lhsT=w_codes[:, w_columns].bitcast(FP8X4),
+                lhsT_scale=w_scales[:, w_columns],
+                rhs=s_codes[:, s_columns].bitcast(FP8X4),
+                rhs_scale=s_scales[:, s_columns],
+                start=True,
+                stop=True,
+            )
+            return bank, bias[:, half * FORMS + j : half * FORMS + j + 1]
+
+        products = {}
+
+        def scalar_forms(group):
+            for k, j in enumerate(SCALAR_FORMS):
+                bank, b = form_pass(group, j)
+                product = chains.tile([P, CHUNK], F32, name="product%d" % k)
+                nc.scalar.activation(out=product[:], in_=bank[:], func=IDENTITY, bias=b, scale=1.0)
+                products[(group, k)] = product
+
+        def vector_form(group, j, k):
+            bank, b = form_pass(group, j)
+            product = products[(group, k)]
+            nc.vector.scalar_tensor_tensor(
+                out=product[:], in0=bank[:], scalar=b, in1=product[:], op0=ADD, op1=MULT
+            )
+
+        def join(group, k):
+            joiner = nc.vector if group == GROUPS - 1 else nc.gpsimd
+            result = products[(group, 0)]
+            joiner.tensor_tensor(out=result[:], in0=result[:], in1=products[(group, k)][:], op=MULT)
+
+        def finish(group):
+            half, chunk = divmod(group, TOKEN_CHUNKS)
+            result = products[(group, 0)]
+            turned = banks.tile([P, CHUNK_ROWS, P], F32, tag="bank")
+            for n in range(CHUNK_ROWS):
+                nc.tensor.transpose(turned[:, n, :], result[:, n * P : (n + 1) * P], identity[:])
+            rows = stage.tile([P, CHUNK_ROWS, P], F32)
+            nc.scalar.copy(out=rows[:], in_=turned[:])
+            nc.sync.dma_start(
+                out=out_rows[:, chunk * CHUNK_ROWS : (chunk + 1) * CHUNK_ROWS, half * P : (half + 1) * P],
+                in_=rows[:],
+            )
+
+        first_units = [
+            ("state", 0, 0),
+            ("state", 0, 1),
+            ("weights", 0, 0),
+            ("weights", 0, 1),
+            ("state", 1, 0),
+            ("state", 1, 1),
+            ("weights", 0, 2),
+            ("weights", 0, 3),
+        ]
+        later_units = {
+            0: [("state", 2, 0), ("state", 2, 1), ("state", 3, 0), ("state", 3, 1)],
+            1: [("weights", 1, 0), ("weights", 1, 1)],
+            2: [("weights", 1, 2), ("weights", 1, 3)],
+        }
+
+        for i in range(len(first_units) + QUANTISE_LAG):
+            if i < len(first_units):
+                mask(first_units[i])
+                turn(first_units[i])
+            if i >= QUANTISE_LAG:
+                quantise(first_units[i - QUANTISE_LAG])
+        scalar_forms(0)
+
+        for group in range(GROUPS):
+            for unit in later_units.get(group, []):
+                mask(unit)
+            for step, (j, k) in enumerate(VECTOR_FORMS):
+                if step == 2:
+                    for unit in later_units.get(group - 1, []):
+                        quantise(unit)
+                vector_form(group, j, k)
+                if j == 6:
+                    join(group, 2)
+                if j == 7:
+                    join(group, 1)
+            if group + 1 < GROUPS:
+                scalar_forms(group + 1)
+            for unit in later_units.get(group, []):
+                turn(unit)
+            if group >= OUT_LAG:
+                finish(group - OUT_LAG)
+        for group in range(GROUPS - OUT_LAG, GROUPS):
+            finish(group)

@@ -90,25 +90,37 @@ def tile_ac_filter_prenorm_net_nd_pa_kernel(tc, state, Wg, Mg, bg, out):
         s_codes = keep.tile([P, TOKENS], U32, align_bytes=64)
         s_scales = keep.tile([P, TOKENS], U8, align_bytes=64)
 
+        masked_tiles = {}
         grouped_tiles = {}
 
         def mask(unit):
             kind, half, pair = unit
             if kind == "weights":
                 w, m = weight_tiles[(half, pair)]
-                nc.vector.tensor_tensor(out=w[:], in0=w[:], in1=m[:], op=MULT)
+                masked = keep.tile([P, 2, UNIT_ROWS * P, 2], BF16, name="masked%d%d" % (half, pair))
+                nc.vector.tensor_tensor(
+                    out=masked[:],
+                    in0=w[:].rearrange("c a (p u e) -> c u (a p) e", u=2, e=2),
+                    in1=m[:].rearrange("c a (p u e) -> c u (a p) e", u=2, e=2),
+                    op=MULT,
+                )
+                masked_tiles[(half, pair)] = masked
 
         def turn(unit):
             kind, i, k = unit
             if kind == "state":
                 rows = state_tiles[i][:, k * UNIT_ROWS : (k + 1) * UNIT_ROWS, :]
+                words = rows.bitcast(F32)
             else:
-                rows = weight_tiles[(i, k)][0][:]
-            words = rows.bitcast(F32)
+                words = masked_tiles[(i, k)][:].rearrange("c u r e -> c u (r e)").bitcast(F32)
             turned = banks.tile([P, UNIT_ROWS, 2, P], F32, tag="bank")
             for a in range(UNIT_ROWS):
                 for u in range(2):
-                    nc.tensor.transpose(turned[:, a, u, :], words[:, a, u : UNIT : 2], identity[:])
+                    if kind == "state":
+                        half_row = words[:, a, u : UNIT : 2]
+                    else:
+                        half_row = words[:, u, a * P : (a + 1) * P]
+                    nc.tensor.transpose(turned[:, a, u, :], half_row, identity[:])
             grouped = keep.tile([P, UNIT_ROWS, P, 4], BF16, name="grouped_%s%d%d" % unit, align_bytes=64)
             nc.scalar.copy(out=grouped[:].bitcast(F32), in_=turned[:].rearrange("p a u r -> p a r u"))
             grouped_tiles[unit] = grouped

@@ -25,11 +25,18 @@ GROUPS = CHANNEL_HALVES * TOKEN_CHUNKS
 UNIT_ROWS = 2
 UNIT = UNIT_ROWS * P
 FORM_PAIRS = FORMS // UNIT_ROWS
-SCALAR_FORMS = (0, 2, 4)
-VECTOR_FORMS = ((1, 0), (3, 1), (5, 2), (6, 0), (7, 1))
 
-QUANTISE_LAG = 3
-OUT_LAG = 2
+
+UNITS = [
+    unit
+    for i in range(TOKENS // UNIT)
+    for unit in (("state",) + divmod(i, CHUNK // UNIT), ("weights",) + divmod(i, FORM_PAIRS))
+]
+MASK_LEAD = 3
+READY_LAG = 2
+FINISH_LAG = 8
+FOUR_PRODUCTS = (0, 1, 2, 3)
+
 
 FLOPS = 2 * TOKENS * CHANNELS * FORMS * E
 
@@ -44,41 +51,31 @@ def tile_ac_filter_prenorm_net_nd_pa_kernel(tc, state, Wg, Mg, bg, out):
     with ExitStack() as ctx:
         ctx.enter_context(tc.manual_schedule())
         keep = ctx.enter_context(tc.tile_pool(name="keep", bufs=1))
-        chains = ctx.enter_context(tc.tile_pool(name="chains", bufs=OUT_LAG + 2))
         stage = ctx.enter_context(tc.tile_pool(name="stage", bufs=3))
         banks = ctx.enter_context(tc.psum_pool(name="banks", bufs=8))
 
         bias_bf16 = keep.tile([P, CHANNEL_HALVES, FORMS], BF16)
         nc.scalar.dma_start(out=bias_bf16[:], in_=bg.rearrange("(h c) j -> c h j", c=P))
 
-        state_tiles = {}
-        weight_tiles = {}
+        loaded = {}
 
-        def load_state(chunk):
-            s = keep.tile([P, CHUNK_ROWS, E], BF16, name="s%d" % chunk)
-            nc.sync.dma_start(
-                out=s[:], in_=state_rows[:, chunk * CHUNK_ROWS : (chunk + 1) * CHUNK_ROWS, :]
-            )
-            state_tiles[chunk] = s
+        def load(unit):
+            kind, i, k = unit
+            if kind == "state":
+                first_row = i * CHUNK_ROWS + k * UNIT_ROWS
+                s = keep.tile([P, UNIT_ROWS, E], BF16, name="s%d%d" % (i, k))
+                nc.sync.dma_start(out=s[:], in_=state_rows[:, first_row : first_row + UNIT_ROWS, :])
+                loaded[unit] = (s,)
+            else:
+                forms = slice(k * UNIT_ROWS, (k + 1) * UNIT_ROWS)
+                w = keep.tile([P, UNIT_ROWS, E], BF16, name="w%d%d" % (i, k))
+                m = keep.tile([P, UNIT_ROWS, E], BF16, name="m%d%d" % (i, k))
+                nc.sync.dma_start(out=w[:], in_=wg_rows[i, :, forms, :])
+                nc.sync.dma_start(out=m[:], in_=mg_rows[i, :, forms, :])
+                loaded[unit] = (w, m)
 
-        def load_weights(half, pair):
-            forms = slice(pair * UNIT_ROWS, (pair + 1) * UNIT_ROWS)
-            w = keep.tile([P, UNIT_ROWS, E], BF16, name="w%d%d" % (half, pair))
-            m = keep.tile([P, UNIT_ROWS, E], BF16, name="m%d%d" % (half, pair))
-            nc.sync.dma_start(out=w[:], in_=wg_rows[half, :, forms, :])
-            nc.sync.dma_start(out=m[:], in_=mg_rows[half, :, forms, :])
-            weight_tiles[(half, pair)] = (w, m)
-
-        load_state(0)
-        load_weights(0, 0)
-        load_weights(0, 1)
-        load_state(1)
-        load_weights(0, 2)
-        load_weights(0, 3)
-        load_state(2)
-        load_state(3)
-        for pair in range(FORM_PAIRS):
-            load_weights(1, pair)
+        for unit in UNITS:
+            load(unit)
 
         identity = keep.tile([P, P], F32)
         make_identity(nc, identity[:])
@@ -94,33 +91,27 @@ def tile_ac_filter_prenorm_net_nd_pa_kernel(tc, state, Wg, Mg, bg, out):
         grouped_tiles = {}
 
         def mask(unit):
-            kind, half, pair = unit
-            if kind == "weights":
-                w, m = weight_tiles[(half, pair)]
-                masked = keep.tile([P, 2, UNIT_ROWS * P, 2], BF16, name="masked%d%d" % (half, pair))
-                nc.vector.tensor_tensor(
-                    out=masked[:],
-                    in0=w[:].rearrange("c a (p u e) -> c u (a p) e", u=2, e=2),
-                    in1=m[:].rearrange("c a (p u e) -> c u (a p) e", u=2, e=2),
-                    op=MULT,
-                )
-                masked_tiles[(half, pair)] = masked
+            w, m = loaded[unit]
+            masked = keep.tile([P, 2, UNIT_ROWS * P, 2], BF16, name="masked%d%d" % unit[1:])
+            nc.vector.tensor_tensor(
+                out=masked[:],
+                in0=w[:].rearrange("c a (p u e) -> c u (a p) e", u=2, e=2),
+                in1=m[:].rearrange("c a (p u e) -> c u (a p) e", u=2, e=2),
+                op=MULT,
+            )
+            masked_tiles[unit] = masked
 
         def turn(unit):
-            kind, i, k = unit
-            if kind == "state":
-                rows = state_tiles[i][:, k * UNIT_ROWS : (k + 1) * UNIT_ROWS, :]
-                words = rows.bitcast(F32)
+            if unit[0] == "state":
+                words = loaded[unit][0][:].bitcast(F32)
+                half_rows = [[words[:, a, u : UNIT : 2] for u in range(2)] for a in range(UNIT_ROWS)]
             else:
-                words = masked_tiles[(i, k)][:].rearrange("c u r e -> c u (r e)").bitcast(F32)
+                words = masked_tiles[unit][:].rearrange("c u r e -> c u (r e)").bitcast(F32)
+                half_rows = [[words[:, u, a * P : (a + 1) * P] for u in range(2)] for a in range(UNIT_ROWS)]
             turned = banks.tile([P, UNIT_ROWS, 2, P], F32, tag="bank")
             for a in range(UNIT_ROWS):
                 for u in range(2):
-                    if kind == "state":
-                        half_row = words[:, a, u : UNIT : 2]
-                    else:
-                        half_row = words[:, u, a * P : (a + 1) * P]
-                    nc.tensor.transpose(turned[:, a, u, :], half_row, identity[:])
+                    nc.tensor.transpose(turned[:, a, u, :], half_rows[a][u], identity[:])
             grouped = keep.tile([P, UNIT_ROWS, P, 4], BF16, name="grouped_%s%d%d" % unit, align_bytes=64)
             nc.scalar.copy(out=grouped[:].bitcast(F32), in_=turned[:].rearrange("p a u r -> p a r u"))
             grouped_tiles[unit] = grouped
@@ -154,12 +145,11 @@ def tile_ac_filter_prenorm_net_nd_pa_kernel(tc, state, Wg, Mg, bg, out):
 
         products = {}
 
-        def scalar_forms(group):
-            for k, j in enumerate(SCALAR_FORMS):
-                bank, b = form_pass(group, j)
-                product = chains.tile([P, CHUNK], F32, name="product%d" % k)
-                nc.scalar.activation(out=product[:], in_=bank[:], func=IDENTITY, bias=b, scale=1.0)
-                products[(group, k)] = product
+        def scalar_form(group, j, k):
+            bank, b = form_pass(group, j)
+            product = keep.tile([P, CHUNK], F32, name="product%d%d" % (group, k))
+            nc.scalar.activation(out=product[:], in_=bank[:], func=IDENTITY, bias=b, scale=1.0)
+            products[(group, k)] = product
 
         def vector_form(group, j, k):
             bank, b = form_pass(group, j)
@@ -168,10 +158,10 @@ def tile_ac_filter_prenorm_net_nd_pa_kernel(tc, state, Wg, Mg, bg, out):
                 out=product[:], in0=bank[:], scalar=b, in1=product[:], op0=ADD, op1=MULT
             )
 
-        def join(group, k):
+        def join(group, a, b):
             joiner = nc.vector if group == GROUPS - 1 else nc.gpsimd
-            result = products[(group, 0)]
-            joiner.tensor_tensor(out=result[:], in0=result[:], in1=products[(group, k)][:], op=MULT)
+            result = products[(group, a)]
+            joiner.tensor_tensor(out=result[:], in0=result[:], in1=products[(group, b)][:], op=MULT)
 
         def finish(group):
             half, chunk = divmod(group, TOKEN_CHUNKS)
@@ -186,47 +176,50 @@ def tile_ac_filter_prenorm_net_nd_pa_kernel(tc, state, Wg, Mg, bg, out):
                 in_=rows[:],
             )
 
-        first_units = [
-            ("state", 0, 0),
-            ("state", 0, 1),
-            ("weights", 0, 0),
-            ("weights", 0, 1),
-            ("state", 1, 0),
-            ("state", 1, 1),
-            ("weights", 0, 2),
-            ("weights", 0, 3),
-        ]
-        later_units = {
-            0: [("state", 2, 0), ("state", 2, 1), ("state", 3, 0), ("state", 3, 1)],
-            1: [("weights", 1, 0), ("weights", 1, 1)],
-            2: [("weights", 1, 2), ("weights", 1, 3)],
-        }
+        def multiply(group, pair):
+            if pair < 3 or group in FOUR_PRODUCTS:
+                scalar_form(group, 2 * pair, pair)
+                vector_form(group, 2 * pair + 1, pair)
+                if group in FOUR_PRODUCTS and pair == 1:
+                    join(group, 0, 1)
+                if pair == 3:
+                    join(group, 2, 3)
+                    join(group, 0, 2)
+            else:
+                vector_form(group, 6, 1)
+                join(group, 0, 1)
+                vector_form(group, 7, 2)
+                join(group, 0, 2)
 
-        for i in range(len(first_units) + QUANTISE_LAG):
-            if i < len(first_units):
-                mask(first_units[i])
-                turn(first_units[i])
-            if i >= QUANTISE_LAG:
-                quantise(first_units[i - QUANTISE_LAG])
-        scalar_forms(0)
+        def ready_step(item):
+            group, pair = item
+            half, chunk = divmod(group, TOKEN_CHUNKS)
+            units = [("state", chunk, 0), ("state", chunk, 1), ("weights", half, pair)]
+            return max([UNITS.index(unit) for unit in units]) + READY_LAG
 
-        for group in range(GROUPS):
-            for unit in later_units.get(group, []):
+        waiting = [(group, pair) for group in range(GROUPS) for pair in range(FORM_PAIRS)]
+        done = []
+        finished = 0
+        for unit in UNITS[:MASK_LEAD]:
+            if unit[0] == "weights":
                 mask(unit)
-            for step, (j, k) in enumerate(VECTOR_FORMS):
-                if step == 2:
-                    for unit in later_units.get(group - 1, []):
-                        quantise(unit)
-                vector_form(group, j, k)
-                if j == 6:
-                    join(group, 2)
-                if j == 7:
-                    join(group, 1)
-            if group + 1 < GROUPS:
-                scalar_forms(group + 1)
-            for unit in later_units.get(group, []):
-                turn(unit)
-            if group >= OUT_LAG:
-                finish(group - OUT_LAG)
-        for group in range(GROUPS - OUT_LAG, GROUPS):
+        step = 0
+        while len(waiting) > 0:
+            preparing = step < len(UNITS)
+            if preparing:
+                turn(UNITS[step])
+            while finished < GROUPS and (finished, FORM_PAIRS - 1) in done[: max(len(done) - FINISH_LAG + 1, 0)]:
+                finish(finished)
+                finished += 1
+            if preparing:
+                quantise(UNITS[step])
+            for unit in UNITS[step + MASK_LEAD : step + MASK_LEAD + 1]:
+                if unit[0] == "weights":
+                    mask(unit)
+            for item in [x for x in waiting if ready_step(x) <= step][: 1 if preparing else FORM_PAIRS]:
+                multiply(*item)
+                waiting.remove(item)
+                done.append(item)
+            step += 1
+        for group in range(finished, GROUPS):
             finish(group)

@@ -26,24 +26,29 @@ UNIT_ROWS = 2
 UNIT = UNIT_ROWS * P
 FORM_PAIRS = FORMS // UNIT_ROWS
 
-
 UNITS = [
     unit
-    for i in range(TOKENS // UNIT)
-    for unit in (("state",) + divmod(i, CHUNK // UNIT), ("weights",) + divmod(i, FORM_PAIRS))
+    for i in range(TOKEN_CHUNKS)
+    for unit in (
+        ("state", i, 0),
+        ("state", i, 1),
+        ("weights",) + divmod(2 * i, FORM_PAIRS),
+        ("weights",) + divmod(2 * i + 1, FORM_PAIRS),
+    )
 ]
 MASK_LEAD = 3
 READY_LAG = 2
-FINISH_LAG = 8
-FOUR_PRODUCTS = (0, 1, 2, 3)
-
+FINISH_LAG = 10
+WARM_FIRST = 3
+WARM_STEPS = 6
+PRODUCTS = (4, 4, 4, 3, 3, 3, 2, 2)
 
 FLOPS = 2 * TOKENS * CHANNELS * FORMS * E
 
 
 def tile_ac_filter_prenorm_net_nd_pa_kernel(tc, state, Wg, Mg, bg, out):
     nc = tc.nc
-    state_rows = state.flatten_outer_dims().rearrange("(q n) e -> q n e", q=P)
+    state_rows = state.flatten_outer_dims().rearrange("(q i n) e -> q i n e", q=P, n=CHUNK_ROWS)
     out_rows = out.flatten_outer_dims().rearrange("(q n) c -> q n c", q=P)
     wg_rows = Wg.rearrange("(h c) j e -> h c j e", c=P)
     mg_rows = Mg.rearrange("(h c) j e -> h c j e", c=P)
@@ -57,26 +62,30 @@ def tile_ac_filter_prenorm_net_nd_pa_kernel(tc, state, Wg, Mg, bg, out):
         bias_bf16 = keep.tile([P, CHANNEL_HALVES, FORMS], BF16)
         nc.scalar.dma_start(out=bias_bf16[:], in_=bg.rearrange("(h c) j -> c h j", c=P))
 
-        loaded = {}
+        rows_of = {}
 
-        def load(unit):
-            kind, i, k = unit
+        def load(name, source, units):
+            tile = keep.tile([P, len(units) * UNIT_ROWS, E], BF16, name=name)
+            nc.sync.dma_start(out=tile[:], in_=source)
+            for i, unit in enumerate(units):
+                rows_of.setdefault(unit, []).append(tile[:, i * UNIT_ROWS : (i + 1) * UNIT_ROWS, :])
+
+        def load_units(units):
+            kind, i, k = units[0]
+            rows = slice(k * UNIT_ROWS, (k + len(units)) * UNIT_ROWS)
             if kind == "state":
-                first_row = i * CHUNK_ROWS + k * UNIT_ROWS
-                s = keep.tile([P, UNIT_ROWS, E], BF16, name="s%d%d" % (i, k))
-                nc.sync.dma_start(out=s[:], in_=state_rows[:, first_row : first_row + UNIT_ROWS, :])
-                loaded[unit] = (s,)
+                load("s%d%d" % (i, k), state_rows[:, i, rows, :], units)
             else:
-                forms = slice(k * UNIT_ROWS, (k + 1) * UNIT_ROWS)
-                w = keep.tile([P, UNIT_ROWS, E], BF16, name="w%d%d" % (i, k))
-                m = keep.tile([P, UNIT_ROWS, E], BF16, name="m%d%d" % (i, k))
-                nc.sync.dma_start(out=w[:], in_=wg_rows[i, :, forms, :])
-                nc.sync.dma_start(out=m[:], in_=mg_rows[i, :, forms, :])
-                loaded[unit] = (w, m)
+                load("w%d%d" % (i, k), wg_rows[i, :, rows, :], units)
+                load("m%d%d" % (i, k), mg_rows[i, :, rows, :], units)
 
-        for unit in UNITS:
-            load(unit)
+        for unit in UNITS[:8]:
+            load_units([unit])
+        for i in range(8, len(UNITS), 2):
+            load_units(UNITS[i : i + 2])
 
+        zeros = keep.tile([P, CHUNK], BF16)
+        nc.gpsimd.memset(zeros[:], 0.0)
         identity = keep.tile([P, P], F32)
         make_identity(nc, identity[:])
         bias = keep.tile([P, CHANNEL_HALVES * FORMS], F32)
@@ -87,23 +96,28 @@ def tile_ac_filter_prenorm_net_nd_pa_kernel(tc, state, Wg, Mg, bg, out):
         s_codes = keep.tile([P, TOKENS], U32, align_bytes=64)
         s_scales = keep.tile([P, TOKENS], U8, align_bytes=64)
 
+        def keep_warm(count):
+            bank = banks.tile([P, CHUNK], F32, tag="bank")
+            for i in range(count):
+                nc.tensor.matmul(out=bank[:], lhsT=zeros[:, :P], rhs=zeros[:], start=True, stop=True)
+
         masked_tiles = {}
         grouped_tiles = {}
 
         def mask(unit):
-            w, m = loaded[unit]
+            w, m = rows_of[unit]
             masked = keep.tile([P, 2, UNIT_ROWS * P, 2], BF16, name="masked%d%d" % unit[1:])
             nc.vector.tensor_tensor(
                 out=masked[:],
-                in0=w[:].rearrange("c a (p u e) -> c u (a p) e", u=2, e=2),
-                in1=m[:].rearrange("c a (p u e) -> c u (a p) e", u=2, e=2),
+                in0=w.rearrange("c a (p u e) -> c u (a p) e", u=2, e=2),
+                in1=m.rearrange("c a (p u e) -> c u (a p) e", u=2, e=2),
                 op=MULT,
             )
             masked_tiles[unit] = masked
 
         def turn(unit):
             if unit[0] == "state":
-                words = loaded[unit][0][:].bitcast(F32)
+                words = rows_of[unit][0].bitcast(F32)
                 half_rows = [[words[:, a, u : UNIT : 2] for u in range(2)] for a in range(UNIT_ROWS)]
             else:
                 words = masked_tiles[unit][:].rearrange("c u r e -> c u (r e)").bitcast(F32)
@@ -151,45 +165,75 @@ def tile_ac_filter_prenorm_net_nd_pa_kernel(tc, state, Wg, Mg, bg, out):
             nc.scalar.activation(out=product[:], in_=bank[:], func=IDENTITY, bias=b, scale=1.0)
             products[(group, k)] = product
 
-        def vector_form(group, j, k):
+        def vector_form(group, j, k, parts=1):
             bank, b = form_pass(group, j)
             product = products[(group, k)]
-            nc.vector.scalar_tensor_tensor(
-                out=product[:], in0=bank[:], scalar=b, in1=product[:], op0=ADD, op1=MULT
-            )
+            for i in range(parts):
+                part = slice(i * CHUNK // parts, (i + 1) * CHUNK // parts)
+                nc.vector.scalar_tensor_tensor(
+                    out=product[:, part], in0=bank[:, part], scalar=b, in1=product[:, part], op0=ADD, op1=MULT
+                )
 
         def join(group, a, b):
-            joiner = nc.vector if group == GROUPS - 1 else nc.gpsimd
             result = products[(group, a)]
-            joiner.tensor_tensor(out=result[:], in0=result[:], in1=products[(group, b)][:], op=MULT)
+            nc.gpsimd.tensor_tensor(out=result[:], in0=result[:], in1=products[(group, b)][:], op=MULT)
+
+        def turn_back(group, k, first, count):
+            turned = banks.tile([P, count, P], F32, tag="bank")
+            for i in range(count):
+                piece = slice((first + i) * P, (first + i + 1) * P)
+                nc.tensor.transpose(turned[:, i, :], products[(group, k)][:, piece], identity[:])
+            return turned
+
+        def store(group, rows, first, count):
+            half, chunk = divmod(group, TOKEN_CHUNKS)
+            n = chunk * CHUNK_ROWS + first
+            nc.sync.dma_start(out=out_rows[:, n : n + count, half * P : (half + 1) * P], in_=rows)
 
         def finish(group):
-            half, chunk = divmod(group, TOKEN_CHUNKS)
-            result = products[(group, 0)]
-            turned = banks.tile([P, CHUNK_ROWS, P], F32, tag="bank")
-            for n in range(CHUNK_ROWS):
-                nc.tensor.transpose(turned[:, n, :], result[:, n * P : (n + 1) * P], identity[:])
+            turned = turn_back(group, 0, 0, CHUNK_ROWS)
             rows = stage.tile([P, CHUNK_ROWS, P], F32)
             nc.scalar.copy(out=rows[:], in_=turned[:])
-            nc.sync.dma_start(
-                out=out_rows[:, chunk * CHUNK_ROWS : (chunk + 1) * CHUNK_ROWS, half * P : (half + 1) * P],
-                in_=rows[:],
-            )
+            store(group, rows[:], 0, CHUNK_ROWS)
 
         def multiply(group, pair):
-            if pair < 3 or group in FOUR_PRODUCTS:
+            if pair < min(PRODUCTS[group], 3):
                 scalar_form(group, 2 * pair, pair)
                 vector_form(group, 2 * pair + 1, pair)
-                if group in FOUR_PRODUCTS and pair == 1:
+            if PRODUCTS[group] == 4:
+                if pair == 1:
                     join(group, 0, 1)
                 if pair == 3:
+                    scalar_form(group, 6, 3)
+                    vector_form(group, 7, 3)
                     join(group, 2, 3)
                     join(group, 0, 2)
-            else:
+            if PRODUCTS[group] == 3 and pair == 3:
                 vector_form(group, 6, 1)
                 join(group, 0, 1)
                 vector_form(group, 7, 2)
                 join(group, 0, 2)
+            if PRODUCTS[group] == 2 and pair == 2:
+                vector_form(group, 4, 0)
+                vector_form(group, 6, 1)
+            if PRODUCTS[group] == 2 and pair == 3:
+                vector_form(group, 5, 0)
+                if group == GROUPS - 1:
+                    vector_form(group, 7, 1, parts=2)
+                else:
+                    vector_form(group, 7, 1)
+                    join(group, 0, 1)
+
+        def finish_last(group):
+            turned = turn_back(group, 0, 0, CHUNK_ROWS)
+            rows = stage.tile([P, CHUNK_ROWS, P], F32)
+            nc.scalar.copy(out=rows[:], in_=turned[:])
+            count = CHUNK_ROWS // 2
+            for first in (0, count):
+                turned = turn_back(group, 1, first, count)
+                part = rows[:, first : first + count, :]
+                nc.vector.tensor_tensor(out=part, in0=turned[:], in1=part, op=MULT)
+                store(group, part, first, count)
 
         def ready_step(item):
             group, pair = item
@@ -200,6 +244,7 @@ def tile_ac_filter_prenorm_net_nd_pa_kernel(tc, state, Wg, Mg, bg, out):
         waiting = [(group, pair) for group in range(GROUPS) for pair in range(FORM_PAIRS)]
         done = []
         finished = 0
+        keep_warm(WARM_FIRST)
         for unit in UNITS[:MASK_LEAD]:
             if unit[0] == "weights":
                 mask(unit)
@@ -208,6 +253,8 @@ def tile_ac_filter_prenorm_net_nd_pa_kernel(tc, state, Wg, Mg, bg, out):
             preparing = step < len(UNITS)
             if preparing:
                 turn(UNITS[step])
+            if step < WARM_STEPS:
+                keep_warm(1)
             while finished < GROUPS and (finished, FORM_PAIRS - 1) in done[: max(len(done) - FINISH_LAG + 1, 0)]:
                 finish(finished)
                 finished += 1
@@ -221,5 +268,6 @@ def tile_ac_filter_prenorm_net_nd_pa_kernel(tc, state, Wg, Mg, bg, out):
                 waiting.remove(item)
                 done.append(item)
             step += 1
-        for group in range(finished, GROUPS):
+        for group in range(finished, GROUPS - 1):
             finish(group)
+        finish_last(GROUPS - 1)

@@ -26,22 +26,19 @@ UNIT_ROWS = 2
 UNIT = UNIT_ROWS * P
 FORM_PAIRS = FORMS // UNIT_ROWS
 
-UNITS = [
-    unit
+STEPS = [
+    step
     for i in range(TOKEN_CHUNKS)
-    for unit in (
-        ("state", i, 0),
-        ("state", i, 1),
-        ("weights",) + divmod(2 * i, FORM_PAIRS),
-        ("weights",) + divmod(2 * i + 1, FORM_PAIRS),
+    for step in (
+        [("state", i, 0), ("state", i, 1)],
+        [("weights",) + divmod(2 * i, FORM_PAIRS), ("weights",) + divmod(2 * i + 1, FORM_PAIRS)],
     )
 ]
-MASK_LEAD = 3
-READY_LAG = 2
-FINISH_LAG = 10
-WARM_FIRST = 3
-WARM_STEPS = 6
-PRODUCTS = (4, 4, 4, 3, 3, 3, 2, 2)
+SINGLE_LOADS = 4
+ITEMS = 3
+LATE_ITEMS = 2
+FINISH_LAG = 12
+PRODUCTS = (4, 4, 3, 3, 3, 3, 2, 2)
 
 FLOPS = 2 * TOKENS * CHANNELS * FORMS * E
 
@@ -58,9 +55,6 @@ def tile_ac_filter_prenorm_net_nd_pa_kernel(tc, state, Wg, Mg, bg, out):
         keep = ctx.enter_context(tc.tile_pool(name="keep", bufs=1))
         stage = ctx.enter_context(tc.tile_pool(name="stage", bufs=3))
         banks = ctx.enter_context(tc.psum_pool(name="banks", bufs=8))
-
-        bias_bf16 = keep.tile([P, CHANNEL_HALVES, FORMS], BF16)
-        nc.scalar.dma_start(out=bias_bf16[:], in_=bg.rearrange("(h c) j -> c h j", c=P))
 
         rows_of = {}
 
@@ -79,27 +73,21 @@ def tile_ac_filter_prenorm_net_nd_pa_kernel(tc, state, Wg, Mg, bg, out):
                 load("w%d%d" % (i, k), wg_rows[i, :, rows, :], units)
                 load("m%d%d" % (i, k), mg_rows[i, :, rows, :], units)
 
-        for unit in UNITS[:8]:
-            load_units([unit])
-        for i in range(8, len(UNITS), 2):
-            load_units(UNITS[i : i + 2])
+        for step, units in enumerate(STEPS):
+            for part in [[unit] for unit in units] if step < SINGLE_LOADS else [units]:
+                load_units(part)
+            if step == 1:
+                bias_bf16 = keep.tile([P, CHANNEL_HALVES, FORMS], BF16)
+                nc.sync.dma_start(out=bias_bf16[:], in_=bg.rearrange("(h c) j -> c h j", c=P))
 
-        zeros = keep.tile([P, CHUNK], BF16)
-        nc.gpsimd.memset(zeros[:], 0.0)
         identity = keep.tile([P, P], F32)
         make_identity(nc, identity[:])
         bias = keep.tile([P, CHANNEL_HALVES * FORMS], F32)
-        nc.vector.tensor_copy(out=bias[:], in_=bias_bf16[:].rearrange("c h j -> c (h j)"))
 
         w_codes = keep.tile([P, CHANNEL_HALVES * FORMS * P], U32, align_bytes=64)
         w_scales = keep.tile([P, CHANNEL_HALVES * FORMS * P], U8, align_bytes=64)
         s_codes = keep.tile([P, TOKENS], U32, align_bytes=64)
         s_scales = keep.tile([P, TOKENS], U8, align_bytes=64)
-
-        def keep_warm(count):
-            bank = banks.tile([P, CHUNK], F32, tag="bank")
-            for i in range(count):
-                nc.tensor.matmul(out=bank[:], lhsT=zeros[:, :P], rhs=zeros[:], start=True, stop=True)
 
         masked_tiles = {}
         grouped_tiles = {}
@@ -238,35 +226,41 @@ def tile_ac_filter_prenorm_net_nd_pa_kernel(tc, state, Wg, Mg, bg, out):
         def ready_step(item):
             group, pair = item
             half, chunk = divmod(group, TOKEN_CHUNKS)
-            units = [("state", chunk, 0), ("state", chunk, 1), ("weights", half, pair)]
-            return max([UNITS.index(unit) for unit in units]) + READY_LAG
+            wanted = [("state", chunk, 0), ("weights", half, pair)]
+            return max([step for step, units in enumerate(STEPS) if any([unit in units for unit in wanted])]) + 1
+
+        def masks(units):
+            for unit in units:
+                if unit[0] == "weights":
+                    mask(unit)
 
         waiting = [(group, pair) for group in range(GROUPS) for pair in range(FORM_PAIRS)]
         done = []
         finished = 0
-        keep_warm(WARM_FIRST)
-        for unit in UNITS[:MASK_LEAD]:
-            if unit[0] == "weights":
-                mask(unit)
         step = 0
         while len(waiting) > 0:
-            preparing = step < len(UNITS)
-            if preparing:
-                turn(UNITS[step])
-            if step < WARM_STEPS:
-                keep_warm(1)
-            while finished < GROUPS and (finished, FORM_PAIRS - 1) in done[: max(len(done) - FINISH_LAG + 1, 0)]:
+            units = STEPS[step] if step < len(STEPS) else []
+            items = [item for item in waiting if ready_step(item) <= step]
+            items = items[: ITEMS if len(units) > 0 else LATE_ITEMS]
+            half_way = (len(items) + 1) // 2
+            for unit in units:
+                turn(unit)
+            if step + 1 < len(STEPS):
+                masks(STEPS[step + 1])
+            if step == 1:
+                nc.vector.tensor_copy(out=bias[:], in_=bias_bf16[:].rearrange("c h j -> c (h j)"))
+            for unit in units:
+                quantise(unit)
+            for item in items[:half_way]:
+                multiply(*item)
+            done.extend(items[:half_way])
+            while finished < GROUPS - 1 and (finished, FORM_PAIRS - 1) in done[: max(len(done) - FINISH_LAG + 1, 0)]:
                 finish(finished)
                 finished += 1
-            if preparing:
-                quantise(UNITS[step])
-            for unit in UNITS[step + MASK_LEAD : step + MASK_LEAD + 1]:
-                if unit[0] == "weights":
-                    mask(unit)
-            for item in [x for x in waiting if ready_step(x) <= step][: 1 if preparing else FORM_PAIRS]:
+            for item in items[half_way:]:
                 multiply(*item)
-                waiting.remove(item)
-                done.append(item)
+            done.extend(items[half_way:])
+            waiting = [item for item in waiting if item not in items]
             step += 1
         for group in range(finished, GROUPS - 1):
             finish(group)

@@ -53,7 +53,7 @@ def tile_ac_filter_prenorm_net_nd_pa_kernel(tc, state, Wg, Mg, bg, out):
     with ExitStack() as ctx:
         ctx.enter_context(tc.manual_schedule())
         keep = ctx.enter_context(tc.tile_pool(name="keep", bufs=1))
-        stage = ctx.enter_context(tc.tile_pool(name="stage", bufs=3))
+        stage = ctx.enter_context(tc.tile_pool(name="stage", bufs=4))
         banks = ctx.enter_context(tc.psum_pool(name="banks", bufs=8))
 
         rows_of = {}
@@ -80,6 +80,8 @@ def tile_ac_filter_prenorm_net_nd_pa_kernel(tc, state, Wg, Mg, bg, out):
                 bias_bf16 = keep.tile([P, CHANNEL_HALVES, FORMS], BF16)
                 nc.sync.dma_start(out=bias_bf16[:], in_=bg.rearrange("(h c) j -> c h j", c=P))
 
+        zeros = keep.tile([P, CHUNK], BF16)
+        nc.gpsimd.memset(zeros[:], 0.0)
         identity = keep.tile([P, P], F32)
         make_identity(nc, identity[:])
         bias = keep.tile([P, CHANNEL_HALVES * FORMS], F32)
@@ -88,6 +90,11 @@ def tile_ac_filter_prenorm_net_nd_pa_kernel(tc, state, Wg, Mg, bg, out):
         w_scales = keep.tile([P, CHANNEL_HALVES * FORMS * P], U8, align_bytes=64)
         s_codes = keep.tile([P, TOKENS], U32, align_bytes=64)
         s_scales = keep.tile([P, TOKENS], U8, align_bytes=64)
+
+        def keep_warm(count):
+            bank = banks.tile([P, CHUNK], F32, tag="bank")
+            for i in range(count):
+                nc.tensor.matmul(out=bank[:], lhsT=zeros[:, :P], rhs=zeros[:], start=True, stop=True)
 
         masked_tiles = {}
         grouped_tiles = {}
@@ -213,15 +220,17 @@ def tile_ac_filter_prenorm_net_nd_pa_kernel(tc, state, Wg, Mg, bg, out):
                     join(group, 0, 1)
 
         def finish_last(group):
-            turned = turn_back(group, 0, 0, CHUNK_ROWS)
-            rows = stage.tile([P, CHUNK_ROWS, P], F32)
-            nc.scalar.copy(out=rows[:], in_=turned[:])
             count = CHUNK_ROWS // 2
+            halves = []
             for first in (0, count):
+                turned = turn_back(group, 0, first, count)
+                rows = stage.tile([P, count, P], F32)
+                nc.scalar.copy(out=rows[:], in_=turned[:])
+                halves.append(rows)
+            for first, rows in zip((0, count), halves):
                 turned = turn_back(group, 1, first, count)
-                part = rows[:, first : first + count, :]
-                nc.vector.tensor_tensor(out=part, in0=turned[:], in1=part, op=MULT)
-                store(group, part, first, count)
+                nc.vector.tensor_tensor(out=rows[:], in0=turned[:], in1=rows[:], op=MULT)
+                store(group, rows[:], first, count)
 
         def ready_step(item):
             group, pair = item
@@ -237,6 +246,7 @@ def tile_ac_filter_prenorm_net_nd_pa_kernel(tc, state, Wg, Mg, bg, out):
         waiting = [(group, pair) for group in range(GROUPS) for pair in range(FORM_PAIRS)]
         done = []
         finished = 0
+        keep_warm(3)
         step = 0
         while len(waiting) > 0:
             units = STEPS[step] if step < len(STEPS) else []
@@ -245,6 +255,8 @@ def tile_ac_filter_prenorm_net_nd_pa_kernel(tc, state, Wg, Mg, bg, out):
             half_way = (len(items) + 1) // 2
             for unit in units:
                 turn(unit)
+                if step == 0:
+                    keep_warm(2)
             if step + 1 < len(STEPS):
                 masks(STEPS[step + 1])
             if step == 1:

from contextlib import ExitStack

import concourse.mybir as mybir
from concourse.masks import make_identity

F32 = mybir.dt.float32
BF16 = mybir.dt.bfloat16
U32 = mybir.dt.uint32
U8 = mybir.dt.uint8
FP8X4 = mybir.dt.float8_e4m3fn_x4
ADD = mybir.AluOpType.add
MULT = mybir.AluOpType.mult
IDENTITY = mybir.ActivationFunctionType.Identity

P = 128
E = 512
TOKENS = 2048
CHANNELS = 256
FORMS = 8
CHUNK = 512
CHUNK_ROWS = CHUNK // P
TOKEN_CHUNKS = TOKENS // CHUNK
CHANNEL_HALVES = CHANNELS // P
GROUPS = CHANNEL_HALVES * TOKEN_CHUNKS
UNIT_ROWS = 2
UNIT = UNIT_ROWS * P
FORM_PAIRS = FORMS // UNIT_ROWS

STEPS = [
    step
    for i in range(TOKEN_CHUNKS)
    for step in (
        [("state", i, 0), ("state", i, 1)],
        [("weights",) + divmod(2 * i, FORM_PAIRS), ("weights",) + divmod(2 * i + 1, FORM_PAIRS)],
    )
]
SINGLE_LOADS = 4
ITEMS = 3
LATE_ITEMS = 2
FINISH_LAG = 12
PRODUCTS = (4, 4, 3, 3, 3, 3, 2, 2)

FLOPS = 2 * TOKENS * CHANNELS * FORMS * E


def tile_ac_filter_prenorm_net_nd_pa_kernel(tc, state, Wg, Mg, bg, out):
    nc = tc.nc
    state_rows = state.flatten_outer_dims().rearrange("(q i n) e -> q i n e", q=P, n=CHUNK_ROWS)
    out_rows = out.flatten_outer_dims().rearrange("(q n) c -> q n c", q=P)
    wg_rows = Wg.rearrange("(h c) j e -> h c j e", c=P)
    mg_rows = Mg.rearrange("(h c) j e -> h c j e", c=P)

    with ExitStack() as ctx:
        ctx.enter_context(tc.manual_schedule())
        keep = ctx.enter_context(tc.tile_pool(name="keep", bufs=1))
        stage = ctx.enter_context(tc.tile_pool(name="stage", bufs=4))
        banks = ctx.enter_context(tc.psum_pool(name="banks", bufs=8))

        rows_of = {}

        def load(name, source, units):
            tile = keep.tile([P, len(units) * UNIT_ROWS, E], BF16, name=name)
            nc.sync.dma_start(out=tile[:], in_=source)
            for i, unit in enumerate(units):
                rows_of.setdefault(unit, []).append(tile[:, i * UNIT_ROWS : (i + 1) * UNIT_ROWS, :])

        def load_units(units):
            kind, i, k = units[0]
            rows = slice(k * UNIT_ROWS, (k + len(units)) * UNIT_ROWS)
            if kind == "state":
                load("s%d%d" % (i, k), state_rows[:, i, rows, :], units)
            else:
                load("w%d%d" % (i, k), wg_rows[i, :, rows, :], units)
                load("m%d%d" % (i, k), mg_rows[i, :, rows, :], units)

        for step, units in enumerate(STEPS):
            for part in [[unit] for unit in units] if step < SINGLE_LOADS else [units]:
                load_units(part)
            if step == 1:
                bias_bf16 = keep.tile([P, CHANNEL_HALVES, FORMS], BF16)
                nc.sync.dma_start(out=bias_bf16[:], in_=bg.rearrange("(h c) j -> c h j", c=P))

        zeros = keep.tile([P, CHUNK], BF16)
        nc.gpsimd.memset(zeros[:], 0.0)
        identity = keep.tile([P, P], F32)
        make_identity(nc, identity[:])
        bias = keep.tile([P, CHANNEL_HALVES * FORMS], F32)

        w_codes = keep.tile([P, CHANNEL_HALVES * FORMS * P], U32, align_bytes=64)
        w_scales = keep.tile([P, CHANNEL_HALVES * FORMS * P], U8, align_bytes=64)
        s_codes = keep.tile([P, TOKENS], U32, align_bytes=64)
        s_scales = keep.tile([P, TOKENS], U8, align_bytes=64)

        def keep_warm(count):
            bank = banks.tile([P, CHUNK], F32, tag="bank")
            for i in range(count):
                nc.tensor.matmul(out=bank[:], lhsT=zeros[:, :P], rhs=zeros[:], start=True, stop=True)

        masked_tiles = {}
        grouped_tiles = {}

        def mask(unit):
            w, m = rows_of[unit]
            masked = keep.tile([P, 2, UNIT_ROWS * P, 2], BF16, name="masked%d%d" % unit[1:])
            nc.vector.tensor_tensor(
                out=masked[:],
                in0=w.rearrange("c a (p u e) -> c u (a p) e", u=2, e=2),
                in1=m.rearrange("c a (p u e) -> c u (a p) e", u=2, e=2),
                op=MULT,
            )
            masked_tiles[unit] = masked

        def turn(unit):
            if unit[0] == "state":
                words = rows_of[unit][0].bitcast(F32)
                half_rows = [[words[:, a, u : UNIT : 2] for u in range(2)] for a in range(UNIT_ROWS)]
            else:
                words = masked_tiles[unit][:].rearrange("c u r e -> c u (r e)").bitcast(F32)
                half_rows = [[words[:, u, a * P : (a + 1) * P] for u in range(2)] for a in range(UNIT_ROWS)]
            turned = banks.tile([P, UNIT_ROWS, 2, P], F32, tag="bank")
            for a in range(UNIT_ROWS):
                for u in range(2):
                    nc.tensor.transpose(turned[:, a, u, :], half_rows[a][u], identity[:])
            grouped = keep.tile([P, UNIT_ROWS, P, 4], BF16, name="grouped_%s%d%d" % unit, align_bytes=64)
            nc.scalar.copy(out=grouped[:].bitcast(F32), in_=turned[:].rearrange("p a u r -> p a r u"))
            grouped_tiles[unit] = grouped

        def quantise(unit):
            kind, i, k = unit
            codes, scales = (s_codes, s_scales) if kind == "state" else (w_codes, w_scales)
            units_before = i * (CHUNK // UNIT) + k if kind == "state" else i * FORM_PAIRS + k
            columns = slice(units_before * UNIT, (units_before + 1) * UNIT)
            nc.vector.quantize_mx(
                out=codes[:, columns].bitcast(FP8X4),
                scales=scales[:, columns],
                in_=grouped_tiles[unit][:].rearrange("p a r t -> p (a r t)"),
            )

        def form_pass(group, j):
            half, chunk = divmod(group, TOKEN_CHUNKS)
            w_columns = slice((half * FORMS + j) * P, (half * FORMS + j + 1) * P)
            s_columns = slice(chunk * CHUNK, (chunk + 1) * CHUNK)
            bank = banks.tile([P, CHUNK], F32, tag="bank")
            nc.tensor.matmul_mx(
                out=bank[:],
                lhsT=w_codes[:, w_columns].bitcast(FP8X4),
                lhsT_scale=w_scales[:, w_columns],
                rhs=s_codes[:, s_columns].bitcast(FP8X4),
                rhs_scale=s_scales[:, s_columns],
                start=True,
                stop=True,
            )
            return bank, bias[:, half * FORMS + j : half * FORMS + j + 1]

        products = {}

        def scalar_form(group, j, k):
            bank, b = form_pass(group, j)
            product = keep.tile([P, CHUNK], F32, name="product%d%d" % (group, k))
            nc.scalar.activation(out=product[:], in_=bank[:], func=IDENTITY, bias=b, scale=1.0)
            products[(group, k)] = product

        def vector_form(group, j, k, parts=1):
            bank, b = form_pass(group, j)
            product = products[(group, k)]
            for i in range(parts):
                part = slice(i * CHUNK // parts, (i + 1) * CHUNK // parts)
                nc.vector.scalar_tensor_tensor(
                    out=product[:, part], in0=bank[:, part], scalar=b, in1=product[:, part], op0=ADD, op1=MULT
                )

        def join(group, a, b):
            result = products[(group, a)]
            nc.gpsimd.tensor_tensor(out=result[:], in0=result[:], in1=products[(group, b)][:], op=MULT)

        def turn_back(group, k, first, count):
            turned = banks.tile([P, count, P], F32, tag="bank")
            for i in range(count):
                piece = slice((first + i) * P, (first + i + 1) * P)
                nc.tensor.transpose(turned[:, i, :], products[(group, k)][:, piece], identity[:])
            return turned

        def store(group, rows, first, count):
            half, chunk = divmod(group, TOKEN_CHUNKS)
            n = chunk * CHUNK_ROWS + first
            nc.sync.dma_start(out=out_rows[:, n : n + count, half * P : (half + 1) * P], in_=rows)

        def finish(group):
            turned = turn_back(group, 0, 0, CHUNK_ROWS)
            rows = stage.tile([P, CHUNK_ROWS, P], F32)
            nc.scalar.copy(out=rows[:], in_=turned[:])
            store(group, rows[:], 0, CHUNK_ROWS)

        def multiply(group, pair):
            if pair < min(PRODUCTS[group], 3):
                scalar_form(group, 2 * pair, pair)
                vector_form(group, 2 * pair + 1, pair)
            if PRODUCTS[group] == 4:
                if pair == 1:
                    join(group, 0, 1)
                if pair == 3:
                    scalar_form(group, 6, 3)
                    vector_form(group, 7, 3)
                    join(group, 2, 3)
                    join(group, 0, 2)
            if PRODUCTS[group] == 3 and pair == 3:
                vector_form(group, 6, 1)
                join(group, 0, 1)
                vector_form(group, 7, 2)
                join(group, 0, 2)
            if PRODUCTS[group] == 2 and pair == 2:
                vector_form(group, 4, 0)
                vector_form(group, 6, 1)
            if PRODUCTS[group] == 2 and pair == 3:
                vector_form(group, 5, 0)
                if group == GROUPS - 1:
                    vector_form(group, 7, 1, parts=2)
                else:
                    vector_form(group, 7, 1)
                    join(group, 0, 1)

        def finish_last(group):
            count = CHUNK_ROWS // 2
            halves = []
            for first in (0, count):
                turned = turn_back(group, 0, first, count)
                rows = stage.tile([P, count, P], F32)
                nc.scalar.copy(out=rows[:], in_=turned[:])
                halves.append(rows)
            for first, rows in zip((0, count), halves):
                turned = turn_back(group, 1, first, count)
                nc.vector.tensor_tensor(out=rows[:], in0=turned[:], in1=rows[:], op=MULT)
                store(group, rows[:], first, count)

        def ready_step(item):
            group, pair = item
            half, chunk = divmod(group, TOKEN_CHUNKS)
            wanted = [("state", chunk, 0), ("weights", half, pair)]
            return max([step for step, units in enumerate(STEPS) if any([unit in units for unit in wanted])]) + 1

        def masks(units):
            for unit in units:
                if unit[0] == "weights":
                    mask(unit)

        waiting = [(group, pair) for group in range(GROUPS) for pair in range(FORM_PAIRS)]
        done = []
        finished = 0
        keep_warm(3)
        step = 0
        while len(waiting) > 0:
            units = STEPS[step] if step < len(STEPS) else []
            items = [item for item in waiting if ready_step(item) <= step]
            items = items[: ITEMS if len(units) > 0 else LATE_ITEMS]
            half_way = (len(items) + 1) // 2
            for unit in units:
                turn(unit)
                if step == 0:
                    keep_warm(2)
            if step + 1 < len(STEPS):
                masks(STEPS[step + 1])
            if step == 1:
                nc.vector.tensor_copy(out=bias[:], in_=bias_bf16[:].rearrange("c h j -> c (h j)"))
            for unit in units:
                quantise(unit)
            for item in items[:half_way]:
                multiply(*item)
            done.extend(items[:half_way])
            while finished < GROUPS - 1 and (finished, FORM_PAIRS - 1) in done[: max(len(done) - FINISH_LAG + 1, 0)]:
                finish(finished)
                finished += 1
            for item in items[half_way:]:
                multiply(*item)
            done.extend(items[half_way:])
            waiting = [item for item in waiting if item not in items]
            step += 1
        for group in range(finished, GROUPS - 1):
            finish(group)
        finish_last(GROUPS - 1)
